import numpy as np
import ml_dtypes


def mxq(x, axis, fmt="e4m3"):
    dtype, down = {"e4m3": (ml_dtypes.float8_e4m3fn, 7), "e5m2": (ml_dtypes.float8_e5m2, 14)}[fmt]
    v = np.moveaxis(np.asarray(x, np.float32).astype(ml_dtypes.bfloat16).astype(np.float64), axis, -1)
    blocks = v.reshape(v.shape[:-1] + (-1, 32))
    amax = np.abs(blocks).max(-1, keepdims=True)
    byte = np.maximum(np.where(amax > 0, np.frexp(amax)[1] - 1 + 127, 0) - down, 1)
    scale = np.exp2(byte - 127.0)
    codes = (blocks / scale).astype(np.float32).astype(dtype).astype(np.float64)
    return np.moveaxis((codes * scale).reshape(v.shape), -1, axis)


WIDE = False


def mx_kscale(k):
    if not WIDE:
        return np.ones(k)
    levels = np.array([10, -10, 5, -5, 0])
    a = np.random.permutation(np.resize(levels, k // 512 * 4)).reshape(k // 512, 4)
    idx = np.arange(k)
    return np.exp2(a[idx // 512, idx % 128 // 32])


BF16 = ml_dtypes.bfloat16


def bf(x):
    return np.asarray(x, np.float32).astype(BF16)


def f64(x):
    return np.asarray(x).astype(np.float64)


E2M1 = np.array([0.0, 0.5, 1.0, 1.5, 2.0, 3.0, 4.0, 6.0, -0.0, -0.5, -1.0, -1.5, -2.0, -3.0, -4.0, -6.0])


def pack_weight(w, fmt):
    k, n = w.shape
    w = f64(bf(w)).reshape(k // 32, 32, n)
    amax = np.abs(w).max(1)
    if fmt == "e4m3":
        byte = np.frexp(amax)[1] - 1 + 127 - 7
    else:
        mant, ex = np.frexp(amax / 6.0)
        byte = np.where(mant > 0.5, ex, ex - 1) + 127
    byte = np.clip(np.where(amax > 0, byte, 1), 1, 254)
    scaled = (w * np.exp2(127.0 - byte)[:, None, :]).reshape(k, n).astype(np.float32)
    by_word = np.ascontiguousarray(scaled.reshape(k // 512, 128, 4, n).transpose(0, 1, 3, 2))
    if fmt == "e4m3":
        words = by_word.astype(ml_dtypes.float8_e4m3fn).view(np.uint8)
    else:
        c = by_word.astype(ml_dtypes.float4_e2m1fn).view(np.uint8) & 0xF
        words = c[..., 0::2] | (c[..., 1::2] << 4)
    return np.ascontiguousarray(words), np.ascontiguousarray(byte.astype(np.uint8).reshape(k // 512, 16, n))


def unpack_weight(words, scales, fmt):
    g, p, n, _ = words.shape
    if fmt == "e4m3":
        vals = np.ascontiguousarray(words).view(ml_dtypes.float8_e4m3fn).astype(np.float64)
    else:
        nib = np.empty((g, p, n, 4), np.uint8)
        nib[..., 0::2] = words & 0xF
        nib[..., 1::2] = words >> 4
        vals = E2M1[nib]
    vals = vals * np.repeat(np.exp2(scales.astype(np.float64) - 127.0), 8, axis=1)[..., None]
    return vals.transpose(0, 1, 3, 2).reshape(g * 512, n)


B, D_IN, HID, OUT = 128, 2048, 4096, 2048


def setup_inputs():
    s, t = mx_kscale(D_IN), mx_kscale(HID)
    u = np.concatenate([s, t])
    x = bf(np.random.standard_normal((B, D_IN)) * s)
    W1 = np.random.standard_normal((HID, D_IN)) / np.sqrt(D_IN) / s[None, :] * t[:, None]
    W1_words, W1_scales = pack_weight(np.ascontiguousarray(W1.T), "e4m3")
    b1 = bf(np.random.standard_normal(HID) * 0.3 * t)
    W2 = np.random.standard_normal((OUT, D_IN + HID)) / np.sqrt(D_IN + HID) / u[None, :]
    W2_words, W2_scales = pack_weight(np.ascontiguousarray(W2.T), "e4m3")
    b2 = bf(np.random.standard_normal(OUT) * 0.3)
    return {"x": x,
            "W1_words": W1_words,
            "W1_scales": W1_scales,
            "b1": b1,
            "W2_words": W2_words,
            "W2_scales": W2_scales,
            "b2": b2}


def reference(x, W1_words, W1_scales, b1, W2_words, W2_scales, b2):
    xq = mxq(f64(x), 1, "e4m3")
    h1 = np.maximum((xq @ unpack_weight(W1_words, W1_scales, "e4m3")) + f64(b1), 0.0)
    concat = np.concatenate([xq, mxq(h1, 1, "e4m3")], axis=1)
    return (concat @ unpack_weight(W2_words, W2_scales, "e4m3")) + f64(b2)

@@ -1,0 +1,198 @@
+from contextlib import ExitStack
+
+import concourse.mybir as mybir
+from concourse.masks import make_identity
+
+FP8X4 = mybir.dt.float8_e4m3fn_x4
+BF16 = mybir.dt.bfloat16
+F32 = mybir.dt.float32
+I32 = mybir.dt.int32
+U32 = mybir.dt.uint32
+U8 = mybir.dt.uint8
+ADD = mybir.AluOpType.add
+RELU = mybir.ActivationFunctionType.Relu
+
+P = 128
+B, D_IN, HID, OUT = 128, 2048, 4096, 2048
+NT = 512
+G1 = D_IN // 512
+GH = HID // 512
+G2 = G1 + GH
+J1 = HID // NT
+J2 = OUT // NT
+
+FLOPS = 2 * B * (D_IN * HID + (D_IN + HID) * OUT)
+
+
+def tile_dpn_w_kernel(tc, x, W1_words, W1_scales, b1, W2_words, W2_scales, b2, out):
+    nc = tc.nc
+    with ExitStack() as ctx:
+        keep = ctx.enter_context(tc.tile_pool(name="keep", bufs=1))
+        psum = ctx.enter_context(tc.psum_pool(name="psum", bufs=1))
+        ctx.enter_context(tc.manual_schedule())
+
+        def bank(i, shape, dtype, name):
+            return psum.tile(shape, dtype, name=name, tag="bank%d" % i)
+
+        x_sb = keep.tile([P, D_IN], BF16, name="x_sb", align_bytes=64)
+        gx = keep.tile([P, D_IN], BF16, name="gx", align_bytes=64)
+        xq = keep.tile([P, G1 * P], U32, name="xq", align_bytes=64)
+        xs = keep.tile([P, G1 * P], U8, name="xs", align_bytes=64)
+        p1 = keep.tile([P, HID], U8, name="p1", align_bytes=64)
+        p2 = [keep.tile([P, OUT], U8, name="p2_%d" % a, align_bytes=64) for a in range(G2 // 4)]
+        w1 = [keep.tile([P, HID], U32, name="w1_%d" % g, align_bytes=64) for g in range(G1)]
+        w2 = [keep.tile([P, OUT], U32, name="w2_%d" % g, align_bytes=64) for g in range(G2 - 1)]
+        w2l = [keep.tile([P, NT], U32, name="w2l_%d" % n, align_bytes=64) for n in range(J2)]
+        ident_f = keep.tile([P, P], F32, name="ident_f")
+        ident_b = keep.tile([P, P], BF16, name="ident_b")
+        bz = keep.tile([P, NT], BF16, name="bz")
+        b1s = keep.tile([P, J1, 4, P], BF16, name="b1s")
+        b2s = keep.tile([P, J2, NT], BF16, name="b2s")
+        hb = [keep.tile([P, 4, P], BF16, name="hb_%d" % j) for j in range(J1)]
+        gh = [keep.tile([P, 2, P, 4], BF16, name="gh_%d" % q, align_bytes=64) for q in range(GH // 2)]
+        hq = [keep.tile([P, 2 * P], U32, name="hq_%d" % q, align_bytes=64) for q in range(GH // 2)]
+        hs = [keep.tile([P, 2 * P], U8, name="hs_%d" % q, align_bytes=64) for q in range(GH // 2)]
+        o_sb = [keep.tile([P, NT], F32, name="o_%d" % n) for n in range(J2)]
+
+        nc.vector.memset(p1[:].bitcast(I32), 0)
+        for a in range(G2 // 4):
+            nc.vector.memset(p2[a][:].bitcast(I32), 0)
+        nc.vector.memset(bz[:], 0.0)
+        make_identity(nc, ident_f[:])
+        make_identity(nc, ident_b[:])
+
+        nc.sync.dma_start(out=x_sb[:], in_=x)
+        nc.scalar.dma_start(out=bz[0:J1, :], in_=b1.rearrange("(r n) -> r n", n=NT))
+        nc.scalar.dma_start(out=bz[J1 : J1 + J2, :], in_=b2.rearrange("(r n) -> r n", n=NT))
+        for q in range(4):
+            nc.sync.dma_start(
+                out=p1[32 * q : 32 * q + 16, :].bitcast(I32),
+                in_=W1_scales[:, 4 * q : 4 * q + 4, :].bitcast(I32),
+            )
+        for a in range(G2 // 4):
+            for q in range(4):
+                nc.sync.dma_start(
+                    out=p2[a][32 * q : 32 * q + 16, :].bitcast(I32),
+                    in_=W2_scales[4 * a : 4 * a + 4, 4 * q : 4 * q + 4, :].bitcast(I32),
+                )
+        for g in range(G1):
+            nc.sync.dma_start(
+                out=w1[g][:].bitcast(I32),
+                in_=W1_words[g].rearrange("p n t -> p (n t)").bitcast(I32),
+            )
+        for g in range(G2 - 1):
+            nc.sync.dma_start(
+                out=w2[g][:].bitcast(I32),
+                in_=W2_words[g].rearrange("p n t -> p (n t)").bitcast(I32),
+            )
+        for n in range(J2):
+            nc.sync.dma_start(
+                out=w2l[n][:].bitcast(I32),
+                in_=W2_words[G2 - 1, :, NT * n : NT * (n + 1), :].rearrange("p n t -> p (n t)").bitcast(I32),
+            )
+
+        xw = x_sb[:].bitcast(F32)
+        gxw = gx[:].bitcast(F32).rearrange("p (g b u) -> p g b u", g=G1, u=2)
+        for half in range(2):
+            xt = bank(half, [P, 2, 2, P], F32, "xt_%d" % half)
+            for gg in range(2):
+                g = 2 * half + gg
+                for u in range(2):
+                    nc.tensor.transpose(xt[:, gg, u, :], xw[:, 256 * g + u : 256 * (g + 1) : 2], ident_f[:])
+            src = xt[:].rearrange("p g u b -> p g b u")
+            dst = gxw[:, 2 * half : 2 * half + 2]
+            if half == 0:
+                nc.vector.tensor_copy(out=dst, in_=src)
+            else:
+                nc.scalar.copy(out=dst, in_=src)
+
+        def spread_bias(r):
+            bb = bank((2 + r) % 8, [P, NT], F32, "bb_%d" % r)
+            nc.tensor.matmul(
+                out=bb[:], lhsT=ident_b[:, r : r + 1].to_broadcast([P, P]), rhs=bz[:], start=True, stop=True
+            )
+            if r < J1:
+                src = bb[:].rearrange("b (p t) -> b t p", t=4)
+                dst = b1s[:, r]
+            else:
+                src = bb[:]
+                dst = b2s[:, r - J1, :]
+            if r % 2 == 0:
+                nc.vector.tensor_copy(out=dst, in_=src)
+            else:
+                nc.scalar.copy(out=dst, in_=src)
+
+        spread_bias(0)
+        spread_bias(1)
+        nc.vector.quantize_mx(out=xq[:].bitcast(FP8X4), scales=xs[:], in_=gx[:])
+        for r in range(2, J1 + J2):
+            spread_bias(r)
+
+        acc1 = [bank(j, [P, NT], F32, "acc1_%d" % j) for j in range(J1)]
+        for g in range(G1):
+            for j in range(J1):
+                nc.tensor.matmul_mx(
+                    out=acc1[j][:],
+                    lhsT=xq[:, P * g : P * (g + 1)].bitcast(FP8X4),
+                    lhsT_scale=xs[:, P * g : P * (g + 1)],
+                    rhs=w1[g][:, NT * j : NT * (j + 1)].bitcast(FP8X4),
+                    rhs_scale=p1[4 * g : P, NT * j : NT * (j + 1)],
+                    start=(g == 0),
+                    stop=(g == G1 - 1),
+                )
+
+        def add_b1(j):
+            nc.vector.tensor_tensor(
+                out=hb[j][:], in0=acc1[j][:].rearrange("b (p t) -> b t p", t=4), in1=b1s[:, j], op=ADD
+            )
+
+        def turn(q):
+            ht = bank(q, [P, 2, 4, P], BF16, "ht_%d" % q)
+            for jj in range(2):
+                for t in range(4):
+                    nc.tensor.transpose(ht[:, jj, t, :], hb[2 * q + jj][:, t, :], ident_b[:])
+            nc.scalar.activation(out=gh[q][:], in_=ht[:].rearrange("p j t b -> p j b t"), func=RELU)
+
+        def quant_h(q):
+            nc.vector.quantize_mx(
+                out=hq[q][:].bitcast(FP8X4), scales=hs[q][:], in_=gh[q][:].rearrange("p j b t -> p (j b t)")
+            )
+
+        for j in range(4):
+            add_b1(j)
+        turn(0)
+        turn(1)
+        add_b1(4)
+        add_b1(5)
+        quant_h(0)
+        add_b1(6)
+        add_b1(7)
+        turn(2)
+        quant_h(1)
+        turn(3)
+        quant_h(2)
+        quant_h(3)
+
+        acc2 = [bank(4 + n, [P, NT], F32, "acc2_%d" % n) for n in range(J2)]
+        for g in range(G2):
+            if g < G1:
+                lhsT = xq[:, P * g : P * (g + 1)]
+                lscale = xs[:, P * g : P * (g + 1)]
+            else:
+                q, jj = divmod(g - G1, 2)
+                lhsT = hq[q][:, P * jj : P * (jj + 1)]
+                lscale = hs[q][:, P * jj : P * (jj + 1)]
+            for n in range(J2):
+                rhs = w2[g][:, NT * n : NT * (n + 1)] if g < G2 - 1 else w2l[n][:]
+                nc.tensor.matmul_mx(
+                    out=acc2[n][:],
+                    lhsT=lhsT.bitcast(FP8X4),
+                    lhsT_scale=lscale,
+                    rhs=rhs.bitcast(FP8X4),
+                    rhs_scale=p2[g // 4][4 * (g % 4) : P, NT * n : NT * (n + 1)],
+                    start=(g == 0),
+                    stop=(g == G2 - 1),
+                )
+        for n in range(J2):
+            nc.vector.tensor_tensor(out=o_sb[n][:], in0=acc2[n][:], in1=b2s[:, n, :], op=ADD)
+            nc.sync.dma_start(out=out[:, NT * n : NT * (n + 1)], in_=o_sb[n][:])

@@ -59,21 +59,21 @@ def tile_dpn_w_kernel(tc, x, W1_words, W1_scales, b1, W2_words, W2_scales, b2, o
             nc.vector.memset(p2[a][:].bitcast(I32), 0)
         nc.vector.memset(bz[:], 0.0)
         make_identity(nc, ident_f[:])
-        make_identity(nc, ident_b[:])
 
         nc.sync.dma_start(out=x_sb[:], in_=x)
         nc.scalar.dma_start(out=bz[0:J1, :], in_=b1.rearrange("(r n) -> r n", n=NT))
         nc.scalar.dma_start(out=bz[J1 : J1 + J2, :], in_=b2.rearrange("(r n) -> r n", n=NT))
         for q in range(4):
-            nc.sync.dma_start(
-                out=p1[32 * q : 32 * q + 16, :].bitcast(I32),
-                in_=W1_scales[:, 4 * q : 4 * q + 4, :].bitcast(I32),
+            nc.gpsimd.dma_start(
+                out=p1[32 * q : 32 * q + 16, :].bitcast(F32),
+                in_=W1_scales[:, 4 * q : 4 * q + 4, :].bitcast(F32),
             )
+        make_identity(nc, ident_b[:])
         for a in range(G2 // 4):
             for q in range(4):
-                nc.sync.dma_start(
-                    out=p2[a][32 * q : 32 * q + 16, :].bitcast(I32),
-                    in_=W2_scales[4 * a : 4 * a + 4, 4 * q : 4 * q + 4, :].bitcast(I32),
+                nc.gpsimd.dma_start(
+                    out=p2[a][32 * q : 32 * q + 16, :].bitcast(F32),
+                    in_=W2_scales[4 * a : 4 * a + 4, 4 * q : 4 * q + 4, :].bitcast(F32),
                 )
         for g in range(G1):
             nc.sync.dma_start(

@@ -20,6 +20,12 @@ GH = HID // 512
 G2 = G1 + GH
 J1 = HID // NT
 J2 = OUT // NT
+BLOCKS = [(0, 512, 4), (512, 512, 5), (1024, 512, 6), (1536, 256, 7), (1792, 256, 0)]
+PIECES = (
+    [(g, 0, 2048) for g in range(9)]
+    + [(9, 0, 1536), (10, 0, 1536), (11, 0, 512), (11, 512, 512), (11, 1024, 512)]
+    + [(9, 1536, 512), (10, 1536, 512), (11, 1536, 256), (11, 1792, 256)]
+)
 
 FLOPS = 2 * B * (D_IN * HID + (D_IN + HID) * OUT)
 
@@ -41,18 +47,17 @@ def tile_dpn_w_kernel(tc, x, W1_words, W1_scales, b1, W2_words, W2_scales, b2, o
         p1 = keep.tile([P, HID], U8, name="p1", align_bytes=64)
         p2 = [keep.tile([P, OUT], U8, name="p2_%d" % a, align_bytes=64) for a in range(G2 // 4)]
         w1 = [keep.tile([P, HID], U32, name="w1_%d" % g, align_bytes=64) for g in range(G1)]
-        w2 = [keep.tile([P, OUT], U32, name="w2_%d" % g, align_bytes=64) for g in range(G2 - 1)]
-        w2l = [keep.tile([P, NT], U32, name="w2l_%d" % n, align_bytes=64) for n in range(J2)]
+        w2 = [keep.tile([P, cn], U32, name="w2_%d_%d" % (g, c0), align_bytes=64) for (g, c0, cn) in PIECES]
         ident_f = keep.tile([P, P], F32, name="ident_f")
         ident_b = keep.tile([P, P], BF16, name="ident_b")
         bz = keep.tile([P, NT], BF16, name="bz")
         b1s = keep.tile([P, J1, 4, P], BF16, name="b1s")
-        b2s = keep.tile([P, J2, NT], BF16, name="b2s")
+        b2s = keep.tile([P, OUT], BF16, name="b2s")
         hb = [keep.tile([P, 4, P], BF16, name="hb_%d" % j) for j in range(J1)]
         gh = [keep.tile([P, 2, P, 4], BF16, name="gh_%d" % q, align_bytes=64) for q in range(GH // 2)]
         hq = [keep.tile([P, 2 * P], U32, name="hq_%d" % q, align_bytes=64) for q in range(GH // 2)]
         hs = [keep.tile([P, 2 * P], U8, name="hs_%d" % q, align_bytes=64) for q in range(GH // 2)]
-        o_sb = [keep.tile([P, NT], F32, name="o_%d" % n) for n in range(J2)]
+        o_sb = [keep.tile([P, bn], F32, name="o_%d" % b0) for (b0, bn, bk) in BLOCKS]
 
         nc.vector.memset(p1[:].bitcast(I32), 0)
         for a in range(G2 // 4):
@@ -80,15 +85,10 @@ def tile_dpn_w_kernel(tc, x, W1_words, W1_scales, b1, W2_words, W2_scales, b2, o
                 out=w1[g][:].bitcast(I32),
                 in_=W1_words[g].rearrange("p n t -> p (n t)").bitcast(I32),
             )
-        for g in range(G2 - 1):
+        for i, (g, c0, cn) in enumerate(PIECES):
             nc.sync.dma_start(
-                out=w2[g][:].bitcast(I32),
-                in_=W2_words[g].rearrange("p n t -> p (n t)").bitcast(I32),
-            )
-        for n in range(J2):
-            nc.sync.dma_start(
-                out=w2l[n][:].bitcast(I32),
-                in_=W2_words[G2 - 1, :, NT * n : NT * (n + 1), :].rearrange("p n t -> p (n t)").bitcast(I32),
+                out=w2[i][:].bitcast(I32),
+                in_=W2_words[g, :, c0 : c0 + cn, :].rearrange("p n t -> p (n t)").bitcast(I32),
             )
 
         xw = x_sb[:].bitcast(F32)
@@ -116,7 +116,7 @@ def tile_dpn_w_kernel(tc, x, W1_words, W1_scales, b1, W2_words, W2_scales, b2, o
                 dst = b1s[:, r]
             else:
                 src = bb[:]
-                dst = b2s[:, r - J1, :]
+                dst = b2s[:, NT * (r - J1) : NT * (r - J1 + 1)]
             if r % 2 == 0:
                 nc.vector.tensor_copy(out=dst, in_=src)
             else:
@@ -173,8 +173,8 @@ def tile_dpn_w_kernel(tc, x, W1_words, W1_scales, b1, W2_words, W2_scales, b2, o
         quant_h(2)
         quant_h(3)
 
-        acc2 = [bank(4 + n, [P, NT], F32, "acc2_%d" % n) for n in range(J2)]
-        for g in range(G2):
+        acc2 = [bank(bk, [P, bn], F32, "acc2_%d" % b0) for (b0, bn, bk) in BLOCKS]
+        for i, (g, c0, cn) in enumerate(PIECES):
             if g < G1:
                 lhsT = xq[:, P * g : P * (g + 1)]
                 lscale = xs[:, P * g : P * (g + 1)]
@@ -182,17 +182,17 @@ def tile_dpn_w_kernel(tc, x, W1_words, W1_scales, b1, W2_words, W2_scales, b2, o
                 q, jj = divmod(g - G1, 2)
                 lhsT = hq[q][:, P * jj : P * (jj + 1)]
                 lscale = hs[q][:, P * jj : P * (jj + 1)]
-            for n in range(J2):
-                rhs = w2[g][:, NT * n : NT * (n + 1)] if g < G2 - 1 else w2l[n][:]
-                nc.tensor.matmul_mx(
-                    out=acc2[n][:],
-                    lhsT=lhsT.bitcast(FP8X4),
-                    lhsT_scale=lscale,
-                    rhs=rhs.bitcast(FP8X4),
-                    rhs_scale=p2[g // 4][4 * (g % 4) : P, NT * n : NT * (n + 1)],
-                    start=(g == 0),
-                    stop=(g == G2 - 1),
-                )
-        for n in range(J2):
-            nc.vector.tensor_tensor(out=o_sb[n][:], in0=acc2[n][:], in1=b2s[:, n, :], op=ADD)
-            nc.sync.dma_start(out=out[:, NT * n : NT * (n + 1)], in_=o_sb[n][:])
+            for k, (b0, bn, bk) in enumerate(BLOCKS):
+                if c0 <= b0 and b0 + bn <= c0 + cn:
+                    nc.tensor.matmul_mx(
+                        out=acc2[k][:],
+                        lhsT=lhsT.bitcast(FP8X4),
+                        lhsT_scale=lscale,
+                        rhs=w2[i][:, b0 - c0 : b0 - c0 + bn].bitcast(FP8X4),
+                        rhs_scale=p2[g // 4][4 * (g % 4) : P, b0 : b0 + bn],
+                        start=(g == 0),
+                        stop=(g == G2 - 1),
+                    )
+        for k, (b0, bn, bk) in enumerate(BLOCKS):
+            nc.vector.tensor_tensor(out=o_sb[k][:], in0=acc2[k][:], in1=b2s[:, b0 : b0 + bn], op=ADD)
+            nc.sync.dma_start(out=out[:, b0 : b0 + bn], in_=o_sb[k][:])

@@ -48,6 +48,7 @@ def tile_dpn_w_kernel(tc, x, W1_words, W1_scales, b1, W2_words, W2_scales, b2, o
         p2 = [keep.tile([P, OUT], U8, name="p2_%d" % a, align_bytes=64) for a in range(G2 // 4)]
         w1 = [keep.tile([P, HID], U32, name="w1_%d" % g, align_bytes=64) for g in range(G1)]
         w2 = [keep.tile([P, cn], U32, name="w2_%d_%d" % (g, c0), align_bytes=64) for (g, c0, cn) in PIECES]
+        pace = keep.tile([P, 8], F32, name="pace")
         ident_f = keep.tile([P, P], F32, name="ident_f")
         ident_b = keep.tile([P, P], BF16, name="ident_b")
         bz = keep.tile([P, NT], BF16, name="bz")
@@ -74,12 +75,6 @@ def tile_dpn_w_kernel(tc, x, W1_words, W1_scales, b1, W2_words, W2_scales, b2, o
                 in_=W1_scales[:, 4 * q : 4 * q + 4, :].bitcast(F32),
             )
         make_identity(nc, ident_b[:])
-        for a in range(G2 // 4):
-            for q in range(4):
-                nc.gpsimd.dma_start(
-                    out=p2[a][32 * q : 32 * q + 16, :].bitcast(F32),
-                    in_=W2_scales[4 * a : 4 * a + 4, 4 * q : 4 * q + 4, :].bitcast(F32),
-                )
         for g in range(G1):
             nc.sync.dma_start(
                 out=w1[g][:].bitcast(I32),
@@ -90,6 +85,14 @@ def tile_dpn_w_kernel(tc, x, W1_words, W1_scales, b1, W2_words, W2_scales, b2, o
                 out=w2[i][:].bitcast(I32),
                 in_=W2_words[g, :, c0 : c0 + cn, :].rearrange("p n t -> p (n t)").bitcast(I32),
             )
+        for n, gate in enumerate([w1[0], w1[1], w1[2], w1[3], w2[0], w2[2]]):
+            nc.gpsimd.tensor_copy(out=pace[:, n : n + 1], in_=gate[:, 0:1].bitcast(F32))
+            a, half = divmod(n, 2)
+            for q in (2 * half, 2 * half + 1):
+                nc.gpsimd.dma_start(
+                    out=p2[a][32 * q : 32 * q + 16, :].bitcast(F32),
+                    in_=W2_scales[4 * a : 4 * a + 4, 4 * q : 4 * q + 4, :].bitcast(F32),
+                )
 
         xw = x_sb[:].bitcast(F32)
         gxw = gx[:].bitcast(F32).rearrange("p (g b u) -> p g b u", g=G1, u=2)

@@ -48,7 +48,6 @@ def tile_dpn_w_kernel(tc, x, W1_words, W1_scales, b1, W2_words, W2_scales, b2, o
         p2 = [keep.tile([P, OUT], U8, name="p2_%d" % a, align_bytes=64) for a in range(G2 // 4)]
         w1 = [keep.tile([P, HID], U32, name="w1_%d" % g, align_bytes=64) for g in range(G1)]
         w2 = [keep.tile([P, cn], U32, name="w2_%d_%d" % (g, c0), align_bytes=64) for (g, c0, cn) in PIECES]
-        pace = keep.tile([P, 8], F32, name="pace")
         ident_f = keep.tile([P, P], F32, name="ident_f")
         ident_b = keep.tile([P, P], BF16, name="ident_b")
         bz = keep.tile([P, NT], BF16, name="bz")
@@ -67,32 +66,36 @@ def tile_dpn_w_kernel(tc, x, W1_words, W1_scales, b1, W2_words, W2_scales, b2, o
         make_identity(nc, ident_f[:])
 
         nc.sync.dma_start(out=x_sb[:], in_=x)
-        nc.scalar.dma_start(out=bz[0:J1, :], in_=b1.rearrange("(r n) -> r n", n=NT))
-        nc.scalar.dma_start(out=bz[J1 : J1 + J2, :], in_=b2.rearrange("(r n) -> r n", n=NT))
         for q in range(4):
             nc.gpsimd.dma_start(
                 out=p1[32 * q : 32 * q + 16, :].bitcast(F32),
                 in_=W1_scales[:, 4 * q : 4 * q + 4, :].bitcast(F32),
             )
         make_identity(nc, ident_b[:])
-        for g in range(G1):
-            nc.sync.dma_start(
-                out=w1[g][:].bitcast(I32),
-                in_=W1_words[g].rearrange("p n t -> p (n t)").bitcast(I32),
-            )
-        for i, (g, c0, cn) in enumerate(PIECES):
-            nc.sync.dma_start(
-                out=w2[i][:].bitcast(I32),
-                in_=W2_words[g, :, c0 : c0 + cn, :].rearrange("p n t -> p (n t)").bitcast(I32),
-            )
-        for n, gate in enumerate([w1[0], w1[1], w1[2], w1[3], w2[0], w2[2]]):
-            nc.gpsimd.tensor_copy(out=pace[:, n : n + 1], in_=gate[:, 0:1].bitcast(F32))
-            a, half = divmod(n, 2)
-            for q in (2 * half, 2 * half + 1):
+        for a in range(G2 // 4):
+            for q in range(4):
                 nc.gpsimd.dma_start(
                     out=p2[a][32 * q : 32 * q + 16, :].bitcast(F32),
                     in_=W2_scales[4 * a : 4 * a + 4, 4 * q : 4 * q + 4, :].bitcast(F32),
                 )
+
+        def load_words(dst, words, second_queue):
+            flat = words.rearrange("p n t -> p (n t)")
+            if second_queue:
+                nc.scalar.dma_start(out=dst[:].bitcast(F32), in_=flat.bitcast(F32))
+            else:
+                nc.sync.dma_start(out=dst[:].bitcast(I32), in_=flat.bitcast(I32))
+
+        def load_piece(i):
+            g, c0, cn = PIECES[i]
+            load_words(w2[i], W2_words[g, :, c0 : c0 + cn, :], i in (1, 3, 5, 7))
+
+        for g in range(G1):
+            load_words(w1[g], W1_words[g], g % 2 == 1)
+        load_piece(0)
+        nc.scalar.dma_start(out=bz[0:J1, :], in_=b1.rearrange("(r n) -> r n", n=NT))
+        nc.scalar.dma_start(out=bz[J1 : J1 + J2, :], in_=b2.rearrange("(r n) -> r n", n=NT))
+        load_piece(1)
 
         xw = x_sb[:].bitcast(F32)
         gxw = gx[:].bitcast(F32).rearrange("p (g b u) -> p g b u", g=G1, u=2)
@@ -108,6 +111,8 @@ def tile_dpn_w_kernel(tc, x, W1_words, W1_scales, b1, W2_words, W2_scales, b2, o
                 nc.vector.tensor_copy(out=dst, in_=src)
             else:
                 nc.scalar.copy(out=dst, in_=src)
+
+        load_piece(2)
 
         def spread_bias(r):
             bb = bank((2 + r) % 8, [P, NT], F32, "bb_%d" % r)
@@ -130,6 +135,8 @@ def tile_dpn_w_kernel(tc, x, W1_words, W1_scales, b1, W2_words, W2_scales, b2, o
         nc.vector.quantize_mx(out=xq[:].bitcast(FP8X4), scales=xs[:], in_=gx[:])
         for r in range(2, J1 + J2):
             spread_bias(r)
+        for i in range(3, len(PIECES)):
+            load_piece(i)
 
         acc1 = [bank(j, [P, NT], F32, "acc1_%d" % j) for j in range(J1)]
         for g in range(G1):

from contextlib import ExitStack

import concourse.mybir as mybir
from concourse.masks import make_identity

FP8X4 = mybir.dt.float8_e4m3fn_x4
BF16 = mybir.dt.bfloat16
F32 = mybir.dt.float32
I32 = mybir.dt.int32
U32 = mybir.dt.uint32
U8 = mybir.dt.uint8
ADD = mybir.AluOpType.add
RELU = mybir.ActivationFunctionType.Relu

P = 128
B, D_IN, HID, OUT = 128, 2048, 4096, 2048
NT = 512
G1 = D_IN // 512
GH = HID // 512
G2 = G1 + GH
J1 = HID // NT
J2 = OUT // NT
BLOCKS = [(0, 512, 4), (512, 512, 5), (1024, 512, 6), (1536, 256, 7), (1792, 256, 0)]
PIECES = (
    [(g, 0, 2048) for g in range(9)]
    + [(9, 0, 1536), (10, 0, 1536), (11, 0, 512), (11, 512, 512), (11, 1024, 512)]
    + [(9, 1536, 512), (10, 1536, 512), (11, 1536, 256), (11, 1792, 256)]
)

FLOPS = 2 * B * (D_IN * HID + (D_IN + HID) * OUT)


def tile_dpn_w_kernel(tc, x, W1_words, W1_scales, b1, W2_words, W2_scales, b2, out):
    nc = tc.nc
    with ExitStack() as ctx:
        keep = ctx.enter_context(tc.tile_pool(name="keep", bufs=1))
        psum = ctx.enter_context(tc.psum_pool(name="psum", bufs=1))
        ctx.enter_context(tc.manual_schedule())

        def bank(i, shape, dtype, name):
            return psum.tile(shape, dtype, name=name, tag="bank%d" % i)

        x_sb = keep.tile([P, D_IN], BF16, name="x_sb", align_bytes=64)
        gx = keep.tile([P, D_IN], BF16, name="gx", align_bytes=64)
        xq = keep.tile([P, G1 * P], U32, name="xq", align_bytes=64)
        xs = keep.tile([P, G1 * P], U8, name="xs", align_bytes=64)
        p1 = keep.tile([P, HID], U8, name="p1", align_bytes=64)
        p2 = [keep.tile([P, OUT], U8, name="p2_%d" % a, align_bytes=64) for a in range(G2 // 4)]
        w1 = [keep.tile([P, HID], U32, name="w1_%d" % g, align_bytes=64) for g in range(G1)]
        w2 = [keep.tile([P, cn], U32, name="w2_%d_%d" % (g, c0), align_bytes=64) for (g, c0, cn) in PIECES]
        ident_f = keep.tile([P, P], F32, name="ident_f")
        ident_b = keep.tile([P, P], BF16, name="ident_b")
        bz = keep.tile([P, NT], BF16, name="bz")
        b1s = keep.tile([P, J1, 4, P], BF16, name="b1s")
        b2s = keep.tile([P, OUT], BF16, name="b2s")
        hb = [keep.tile([P, 4, P], BF16, name="hb_%d" % j) for j in range(J1)]
        gh = [keep.tile([P, 2, P, 4], BF16, name="gh_%d" % q, align_bytes=64) for q in range(GH // 2)]
        hq = [keep.tile([P, 2 * P], U32, name="hq_%d" % q, align_bytes=64) for q in range(GH // 2)]
        hs = [keep.tile([P, 2 * P], U8, name="hs_%d" % q, align_bytes=64) for q in range(GH // 2)]
        o_sb = [keep.tile([P, bn], F32, name="o_%d" % b0) for (b0, bn, bk) in BLOCKS]

        nc.vector.memset(p1[:].bitcast(I32), 0)
        for a in range(G2 // 4):
            nc.vector.memset(p2[a][:].bitcast(I32), 0)
        nc.vector.memset(bz[:], 0.0)
        make_identity(nc, ident_f[:])

        nc.sync.dma_start(out=x_sb[:], in_=x)
        for q in range(4):
            nc.gpsimd.dma_start(
                out=p1[32 * q : 32 * q + 16, :].bitcast(F32),
                in_=W1_scales[:, 4 * q : 4 * q + 4, :].bitcast(F32),
            )
        make_identity(nc, ident_b[:])
        for a in range(G2 // 4):
            for q in range(4):
                nc.gpsimd.dma_start(
                    out=p2[a][32 * q : 32 * q + 16, :].bitcast(F32),
                    in_=W2_scales[4 * a : 4 * a + 4, 4 * q : 4 * q + 4, :].bitcast(F32),
                )

        def load_words(dst, words, second_queue):
            flat = words.rearrange("p n t -> p (n t)")
            if second_queue:
                nc.scalar.dma_start(out=dst[:].bitcast(F32), in_=flat.bitcast(F32))
            else:
                nc.sync.dma_start(out=dst[:].bitcast(I32), in_=flat.bitcast(I32))

        def load_piece(i):
            g, c0, cn = PIECES[i]
            load_words(w2[i], W2_words[g, :, c0 : c0 + cn, :], i in (1, 3, 5, 7))

        for g in range(G1):
            load_words(w1[g], W1_words[g], g % 2 == 1)
        load_piece(0)
        nc.scalar.dma_start(out=bz[0:J1, :], in_=b1.rearrange("(r n) -> r n", n=NT))
        nc.scalar.dma_start(out=bz[J1 : J1 + J2, :], in_=b2.rearrange("(r n) -> r n", n=NT))
        load_piece(1)

        xw = x_sb[:].bitcast(F32)
        gxw = gx[:].bitcast(F32).rearrange("p (g b u) -> p g b u", g=G1, u=2)
        for half in range(2):
            xt = bank(half, [P, 2, 2, P], F32, "xt_%d" % half)
            for gg in range(2):
                g = 2 * half + gg
                for u in range(2):
                    nc.tensor.transpose(xt[:, gg, u, :], xw[:, 256 * g + u : 256 * (g + 1) : 2], ident_f[:])
            src = xt[:].rearrange("p g u b -> p g b u")
            dst = gxw[:, 2 * half : 2 * half + 2]
            if half == 0:
                nc.vector.tensor_copy(out=dst, in_=src)
            else:
                nc.scalar.copy(out=dst, in_=src)

        load_piece(2)

        def spread_bias(r):
            bb = bank((2 + r) % 8, [P, NT], F32, "bb_%d" % r)
            nc.tensor.matmul(
                out=bb[:], lhsT=ident_b[:, r : r + 1].to_broadcast([P, P]), rhs=bz[:], start=True, stop=True
            )
            if r < J1:
                src = bb[:].rearrange("b (p t) -> b t p", t=4)
                dst = b1s[:, r]
            else:
                src = bb[:]
                dst = b2s[:, NT * (r - J1) : NT * (r - J1 + 1)]
            if r % 2 == 0:
                nc.vector.tensor_copy(out=dst, in_=src)
            else:
                nc.scalar.copy(out=dst, in_=src)

        spread_bias(0)
        spread_bias(1)
        nc.vector.quantize_mx(out=xq[:].bitcast(FP8X4), scales=xs[:], in_=gx[:])
        for r in range(2, J1 + J2):
            spread_bias(r)
        for i in range(3, len(PIECES)):
            load_piece(i)

        acc1 = [bank(j, [P, NT], F32, "acc1_%d" % j) for j in range(J1)]
        for g in range(G1):
            for j in range(J1):
                nc.tensor.matmul_mx(
                    out=acc1[j][:],
                    lhsT=xq[:, P * g : P * (g + 1)].bitcast(FP8X4),
                    lhsT_scale=xs[:, P * g : P * (g + 1)],
                    rhs=w1[g][:, NT * j : NT * (j + 1)].bitcast(FP8X4),
                    rhs_scale=p1[4 * g : P, NT * j : NT * (j + 1)],
                    start=(g == 0),
                    stop=(g == G1 - 1),
                )

        def add_b1(j):
            nc.vector.tensor_tensor(
                out=hb[j][:], in0=acc1[j][:].rearrange("b (p t) -> b t p", t=4), in1=b1s[:, j], op=ADD
            )

        def turn(q):
            ht = bank(q, [P, 2, 4, P], BF16, "ht_%d" % q)
            for jj in range(2):
                for t in range(4):
                    nc.tensor.transpose(ht[:, jj, t, :], hb[2 * q + jj][:, t, :], ident_b[:])
            nc.scalar.activation(out=gh[q][:], in_=ht[:].rearrange("p j t b -> p j b t"), func=RELU)

        def quant_h(q):
            nc.vector.quantize_mx(
                out=hq[q][:].bitcast(FP8X4), scales=hs[q][:], in_=gh[q][:].rearrange("p j b t -> p (j b t)")
            )

        for j in range(4):
            add_b1(j)
        turn(0)
        turn(1)
        add_b1(4)
        add_b1(5)
        quant_h(0)
        add_b1(6)
        add_b1(7)
        turn(2)
        quant_h(1)
        turn(3)
        quant_h(2)
        quant_h(3)

        acc2 = [bank(bk, [P, bn], F32, "acc2_%d" % b0) for (b0, bn, bk) in BLOCKS]
        for i, (g, c0, cn) in enumerate(PIECES):
            if g < G1:
                lhsT = xq[:, P * g : P * (g + 1)]
                lscale = xs[:, P * g : P * (g + 1)]
            else:
                q, jj = divmod(g - G1, 2)
                lhsT = hq[q][:, P * jj : P * (jj + 1)]
                lscale = hs[q][:, P * jj : P * (jj + 1)]
            for k, (b0, bn, bk) in enumerate(BLOCKS):
                if c0 <= b0 and b0 + bn <= c0 + cn:
                    nc.tensor.matmul_mx(
                        out=acc2[k][:],
                        lhsT=lhsT.bitcast(FP8X4),
                        lhsT_scale=lscale,
                        rhs=w2[i][:, b0 - c0 : b0 - c0 + bn].bitcast(FP8X4),
                        rhs_scale=p2[g // 4][4 * (g % 4) : P, b0 : b0 + bn],
                        start=(g == 0),
                        stop=(g == G2 - 1),
                    )
        for k, (b0, bn, bk) in enumerate(BLOCKS):
            nc.vector.tensor_tensor(out=o_sb[k][:], in0=acc2[k][:], in1=b2s[:, b0 : b0 + bn], op=ADD)
            nc.sync.dma_start(out=out[:, b0 : b0 + bn], in_=o_sb[k][:])
